import numpy as np
import ml_dtypes


def mxq(x, axis, fmt="e4m3"):
    dtype, down = {"e4m3": (ml_dtypes.float8_e4m3fn, 7), "e5m2": (ml_dtypes.float8_e5m2, 14)}[fmt]
    v = np.moveaxis(np.asarray(x, np.float32).astype(ml_dtypes.bfloat16).astype(np.float64), axis, -1)
    blocks = v.reshape(v.shape[:-1] + (-1, 32))
    amax = np.abs(blocks).max(-1, keepdims=True)
    byte = np.maximum(np.where(amax > 0, np.frexp(amax)[1] - 1 + 127, 0) - down, 1)
    scale = np.exp2(byte - 127.0)
    codes = (blocks / scale).astype(np.float32).astype(dtype).astype(np.float64)
    return np.moveaxis((codes * scale).reshape(v.shape), -1, axis)


WIDE = False


def mx_kscale(k):
    if not WIDE:
        return np.ones(k)
    levels = np.array([10, -10, 5, -5, 0])
    a = np.random.permutation(np.resize(levels, k // 512 * 4)).reshape(k // 512, 4)
    idx = np.arange(k)
    return np.exp2(a[idx // 512, idx % 128 // 32])


BF16 = ml_dtypes.bfloat16


def bf(x):
    return np.asarray(x, np.float32).astype(BF16)


def f64(x):
    return np.asarray(x).astype(np.float64)


E2M1 = np.array([0.0, 0.5, 1.0, 1.5, 2.0, 3.0, 4.0, 6.0, -0.0, -0.5, -1.0, -1.5, -2.0, -3.0, -4.0, -6.0])


def pack_weight(w, fmt):
    k, n = w.shape
    w = f64(bf(w)).reshape(k // 32, 32, n)
    amax = np.abs(w).max(1)
    if fmt == "e4m3":
        byte = np.frexp(amax)[1] - 1 + 127 - 7
    else:
        mant, ex = np.frexp(amax / 6.0)
        byte = np.where(mant > 0.5, ex, ex - 1) + 127
    byte = np.clip(np.where(amax > 0, byte, 1), 1, 254)
    scaled = (w * np.exp2(127.0 - byte)[:, None, :]).reshape(k, n).astype(np.float32)
    by_word = np.ascontiguousarray(scaled.reshape(k // 512, 128, 4, n).transpose(0, 1, 3, 2))
    if fmt == "e4m3":
        words = by_word.astype(ml_dtypes.float8_e4m3fn).view(np.uint8)
    else:
        c = by_word.astype(ml_dtypes.float4_e2m1fn).view(np.uint8) & 0xF
        words = c[..., 0::2] | (c[..., 1::2] << 4)
    return np.ascontiguousarray(words), np.ascontiguousarray(byte.astype(np.uint8).reshape(k // 512, 16, n))


def unpack_weight(words, scales, fmt):
    g, p, n, _ = words.shape
    if fmt == "e4m3":
        vals = np.ascontiguousarray(words).view(ml_dtypes.float8_e4m3fn).astype(np.float64)
    else:
        nib = np.empty((g, p, n, 4), np.uint8)
        nib[..., 0::2] = words & 0xF
        nib[..., 1::2] = words >> 4
        vals = E2M1[nib]
    vals = vals * np.repeat(np.exp2(scales.astype(np.float64) - 127.0), 8, axis=1)[..., None]
    return vals.transpose(0, 1, 3, 2).reshape(g * 512, n)


B, S, D, H, HD, M, G = 4, 2048, 512, 1, 128, 4096, 3
EPS = 1e-6


def rmsnorm(x, gain):
    var = np.mean(np.square(x), axis=-1, keepdims=True)
    return x * (1.0 / np.sqrt(var + EPS)) * gain


def setup_inputs():
    s = mx_kscale(D)
    x = bf(np.random.standard_normal((B, S, D)))
    rms1_scale = bf((1.0 + 0.1 * np.random.standard_normal(D)) * s)
    words, scales = pack_weight(np.random.standard_normal((D, G * H * HD)) / np.sqrt(D) / s[:, None], "e4m3")
    return {"x": x,
            "rms1_scale": rms1_scale,
            "w_qkv_words": words,
            "w_qkv_scales": scales}


def reference(x, rms1_scale, w_qkv_words, w_qkv_scales):
    h = rmsnorm(f64(x), f64(rms1_scale))
    qkv = mxq(h, 2, "e4m3") @ unpack_weight(w_qkv_words, w_qkv_scales, "e4m3")
    qkv = qkv.reshape(B, S, G, H, HD)
    return qkv[:, :, 0], qkv[:, :, 1], qkv[:, :, 2]

@@ -1,0 +1,198 @@
+from contextlib import ExitStack
+
+import concourse.mybir as mybir
+from concourse.masks import make_identity
+
+F32 = mybir.dt.float32
+BF16 = mybir.dt.bfloat16
+I32 = mybir.dt.int32
+U32 = mybir.dt.uint32
+U8 = mybir.dt.uint8
+FP8X4 = mybir.dt.float8_e4m3fn_x4
+ALU = mybir.AluOpType
+ACT = mybir.ActivationFunctionType
+
+P = 128
+PACK = 4
+FEATURES = P * PACK
+HEAD = 128
+PROJECTIONS = 3
+N_OUT = PROJECTIONS * HEAD
+TOKENS = 4 * 2048
+TILES = TOKENS // P
+GROUP = 4
+GROUPS = TILES // GROUP
+EPS = 1e-6
+
+FLOPS = 2 * TOKENS * FEATURES * N_OUT
+
+
+def tile_transformerblocktpu_pa_t_kernel(
+    tc, x, rms1_scale, w_qkv_words, w_qkv_scales, out_0, out_1, out_2
+):
+    nc = tc.nc
+    x_rows = x.rearrange("b (q j) k -> (b q) j k", j=TILES)
+    out_rows = [
+        o.rearrange("b (q j) h d -> (b q) j (h d)", j=TILES) for o in (out_0, out_1, out_2)
+    ]
+
+    with ExitStack() as ctx:
+        ctx.enter_context(tc.manual_schedule())
+        const = ctx.enter_context(tc.tile_pool(name="const", bufs=1))
+        x_pool = ctx.enter_context(tc.tile_pool(name="x", bufs=GROUPS))
+        junk_pool = ctx.enter_context(tc.tile_pool(name="junk", bufs=4))
+        stat_pool = ctx.enter_context(tc.tile_pool(name="stat", bufs=6))
+        y_pool = ctx.enter_context(tc.tile_pool(name="y", bufs=2 * GROUP))
+        h_pool = ctx.enter_context(tc.tile_pool(name="h", bufs=2))
+        q_pool = ctx.enter_context(tc.tile_pool(name="q", bufs=3))
+        o_pool = ctx.enter_context(tc.tile_pool(name="o", bufs=4))
+        psum_t = ctx.enter_context(tc.psum_pool(name="psum_t", bufs=GROUP))
+        psum_o = ctx.enter_context(tc.psum_pool(name="psum_o", bufs=GROUP))
+
+        x_tiles = {}
+        rms_tiles = {}
+        rstd_tiles = {}
+        y_tiles = {}
+        yT_tiles = {}
+        h_tiles = {}
+        code_tiles = {}
+        plane_tiles = {}
+        acc_tiles = {}
+        stage_tiles = {}
+
+        def load(g):
+            x_g = x_pool.tile([P, GROUP, FEATURES], BF16)
+            nc.sync.dma_start(out=x_g[:], in_=x_rows[:, g * GROUP : (g + 1) * GROUP, :])
+            x_tiles[g] = x_g
+
+        load(0)
+        gain = const.tile([P, PACK], BF16)
+        nc.sync.dma_start(out=gain[:], in_=rms1_scale.rearrange("(c t) -> c t", t=PACK))
+        w_codes = const.tile([P, PACK * N_OUT], U8, align_bytes=64)
+        nc.sync.dma_start(
+            out=w_codes[:].bitcast(I32),
+            in_=w_qkv_words[0].rearrange("p n t -> p (n t)").bitcast(I32),
+        )
+        w_plane = const.tile([P, N_OUT], U8, align_bytes=64)
+        nc.vector.memset(w_plane[:].bitcast(I32), 0)
+        for quadrant in range(4):
+            nc.sync.dma_start(
+                out=w_plane[32 * quadrant : 32 * quadrant + 4, :].bitcast(I32),
+                in_=w_qkv_scales[0, 4 * quadrant : 4 * quadrant + 4, :].bitcast(I32),
+            )
+        for g in range(1, GROUPS):
+            load(g)
+        eps = const.tile([P, 1], F32)
+        nc.vector.memset(eps[:], EPS)
+        warm = const.tile([P, 1], F32)
+        nc.scalar.activation(out=warm[:], in_=eps[:], func=ACT.Sqrt)
+        ident = const.tile([P, P], F32)
+        make_identity(nc, ident[:])
+
+        def statistics(g):
+            sumsq = stat_pool.tile([P, GROUP], F32)
+            for j in range(GROUP):
+                junk = junk_pool.tile([P, FEATURES], BF16)
+                nc.scalar.activation(
+                    out=junk[:],
+                    in_=x_tiles[g][:, j, :],
+                    func=ACT.Square,
+                    accum_out=sumsq[:, j : j + 1],
+                )
+            rms = stat_pool.tile([P, GROUP], F32)
+            nc.scalar.activation(
+                out=rms[:], in_=sumsq[:], func=ACT.Sqrt, scale=1.0 / FEATURES, bias=eps[:]
+            )
+            rms_tiles[g] = rms
+
+        def scale_rows(g):
+            rstd = stat_pool.tile([P, GROUP], F32)
+            nc.vector.reciprocal(out=rstd[:], in_=rms_tiles[g][:])
+            rstd_tiles[g] = rstd
+            for j in range(GROUP):
+                y = y_pool.tile([P, PACK, P], F32)
+                nc.vector.tensor_scalar(
+                    out=y[:],
+                    in0=x_tiles[g][:, j, :].rearrange("r (c t) -> r t c", t=PACK),
+                    scalar1=rstd[:, j : j + 1],
+                    scalar2=None,
+                    op0=ALU.mult,
+                )
+                y_tiles[(g, j)] = y
+
+        def transpose(g):
+            for j in range(GROUP):
+                yT = psum_t.tile([P, PACK, P], F32)
+                for t in range(PACK):
+                    nc.tensor.transpose(yT[:, t, :], y_tiles[(g, j)][:, t, :], ident[:])
+                yT_tiles[(g, j)] = yT
+
+        def apply_gain(g):
+            h = h_pool.tile([P, GROUP, P, PACK], BF16, align_bytes=64)
+            for j in range(GROUP):
+                nc.vector.tensor_tensor(
+                    out=h[:, j, :, :],
+                    in0=yT_tiles[(g, j)][:].rearrange("c t r -> c r t"),
+                    in1=gain[:].unsqueeze(1).to_broadcast([P, P, PACK]),
+                    op=ALU.mult,
+                )
+            h_tiles[g] = h
+
+        def quantise(g):
+            codes = q_pool.tile([P, GROUP * P], U32, align_bytes=64)
+            plane = q_pool.tile([P, GROUP * P], U8, align_bytes=64)
+            nc.vector.quantize_mx(
+                out=codes[:].bitcast(FP8X4),
+                scales=plane[:],
+                in_=h_tiles[g][:].rearrange("c j r t -> c (j r t)"),
+            )
+            code_tiles[g] = codes
+            plane_tiles[g] = plane
+
+        def project(g):
+            for j in range(GROUP):
+                acc = psum_o.tile([P, N_OUT], F32)
+                rows = slice(j * P, (j + 1) * P)
+                for lo, hi in ((0, 256), (256, N_OUT)):
+                    nc.tensor.matmul_mx(
+                        out=acc[:, lo:hi],
+                        lhsT=code_tiles[g][:, rows].bitcast(FP8X4),
+                        lhsT_scale=plane_tiles[g][:, rows],
+                        rhs=w_codes[:, PACK * lo : PACK * hi].bitcast(FP8X4),
+                        rhs_scale=w_plane[:, lo:hi],
+                        start=True,
+                        stop=True,
+                    )
+                acc_tiles[(g, j)] = acc
+
+        def evacuate(g):
+            stage = o_pool.tile([P, PROJECTIONS, GROUP, HEAD], F32)
+            for j in range(GROUP):
+                nc.scalar.copy(
+                    out=stage[:, :, j, :],
+                    in_=acc_tiles[(g, j)][:].rearrange("r (i d) -> r i d", i=PROJECTIONS),
+                )
+            stage_tiles[g] = stage
+
+        def store(g):
+            for i in range(PROJECTIONS):
+                nc.sync.dma_start(
+                    out=out_rows[i][:, g * GROUP : (g + 1) * GROUP, :],
+                    in_=stage_tiles[g][:, i, :, :],
+                )
+
+        for step in range(-3, GROUPS):
+            if step >= 0:
+                apply_gain(step)
+            if 0 <= step + 1 < GROUPS:
+                transpose(step + 1)
+            if 0 <= step + 2 < GROUPS:
+                scale_rows(step + 2)
+            if step >= 0:
+                quantise(step)
+                project(step)
+            if step + 3 < GROUPS:
+                statistics(step + 3)
+            if step >= 0:
+                evacuate(step)
+                store(step)

@@ -22,6 +22,7 @@ TOKENS = 4 * 2048
 TILES = TOKENS // P
 GROUP = 4
 GROUPS = TILES // GROUP
+VECTOR_TILE = GROUP - 1
 EPS = 1e-6
 
 FLOPS = 2 * TOKENS * FEATURES * N_OUT
@@ -111,13 +112,20 @@ def tile_transformerblocktpu_pa_t_kernel(
             rstd_tiles[g] = rstd
             for j in range(GROUP):
                 y = y_pool.tile([P, PACK, P], F32)
-                nc.vector.tensor_scalar(
-                    out=y[:],
-                    in0=x_tiles[g][:, j, :].rearrange("r (c t) -> r t c", t=PACK),
-                    scalar1=rstd[:, j : j + 1],
-                    scalar2=None,
-                    op0=ALU.mult,
-                )
+                sorted_x = x_tiles[g][:, j, :].rearrange("r (c t) -> r t c", t=PACK)
+                if j == VECTOR_TILE:
+                    nc.vector.tensor_scalar(
+                        out=y[:], in0=sorted_x, scalar1=rstd[:, j : j + 1], scalar2=None, op0=ALU.mult
+                    )
+                else:
+                    nc.gpsimd.tensor_scalar(
+                        out=y[:],
+                        in0=sorted_x,
+                        scalar1=rstd[:, j : j + 1],
+                        scalar2=0.0,
+                        op0=ALU.mult,
+                        op1=ALU.add,
+                    )
                 y_tiles[(g, j)] = y
 
         def transpose(g):
@@ -168,7 +176,8 @@ def tile_transformerblocktpu_pa_t_kernel(
         def evacuate(g):
             stage = o_pool.tile([P, PROJECTIONS, GROUP, HEAD], F32)
             for j in range(GROUP):
-                nc.scalar.copy(
+                copy = nc.vector.tensor_copy if j == VECTOR_TILE else nc.scalar.copy
+                copy(
                     out=stage[:, :, j, :],
                     in_=acc_tiles[(g, j)][:].rearrange("r (i d) -> r i d", i=PROJECTIONS),
                 )
@@ -181,18 +190,18 @@ def tile_transformerblocktpu_pa_t_kernel(
                     in_=stage_tiles[g][:, i, :, :],
                 )
 
-        for step in range(-3, GROUPS):
-            if step >= 0:
+        for step in range(-3, GROUPS + 1):
+            if 0 <= step < GROUPS:
                 apply_gain(step)
             if 0 <= step + 1 < GROUPS:
                 transpose(step + 1)
-            if 0 <= step + 2 < GROUPS:
-                scale_rows(step + 2)
-            if step >= 0:
+            if step >= 1:
+                evacuate(step - 1)
+                store(step - 1)
+            if 0 <= step < GROUPS:
                 quantise(step)
                 project(step)
+            if 0 <= step + 2 < GROUPS:
+                scale_rows(step + 2)
             if step + 3 < GROUPS:
                 statistics(step + 3)
-            if step >= 0:
-                evacuate(step)
-                store(step)

@@ -21,17 +21,29 @@ N_OUT = PROJECTIONS * HEAD
 TOKENS = 4 * 2048
 TILES = TOKENS // P
 GROUP = 4
-GROUPS = TILES // GROUP
-VECTOR_TILE = GROUP - 1
 EPS = 1e-6
+SCALE_LEAD = 2
+STATS_LEAD = 3
 
 FLOPS = 2 * TOKENS * FEATURES * N_OUT
+
+
+def group_sizes():
+    ramp = [1]
+    while sum(ramp) < GROUP:
+        ramp.append(sum(ramp))
+    full = [GROUP] * ((TILES - 2 * sum(ramp)) // GROUP)
+    return ramp + full + list(reversed(ramp))
 
 
 def tile_transformerblocktpu_pa_t_kernel(
     tc, x, rms1_scale, w_qkv_words, w_qkv_scales, out_0, out_1, out_2
 ):
     nc = tc.nc
+    sizes = group_sizes()
+    groups = len(sizes)
+    firsts = [sum(sizes[:g]) for g in range(groups)]
+
     x_rows = x.rearrange("b (q j) k -> (b q) j k", j=TILES)
     out_rows = [
         o.rearrange("b (q j) h d -> (b q) j (h d)", j=TILES) for o in (out_0, out_1, out_2)
@@ -40,7 +52,7 @@ def tile_transformerblocktpu_pa_t_kernel(
     with ExitStack() as ctx:
         ctx.enter_context(tc.manual_schedule())
         const = ctx.enter_context(tc.tile_pool(name="const", bufs=1))
-        x_pool = ctx.enter_context(tc.tile_pool(name="x", bufs=GROUPS))
+        x_pool = ctx.enter_context(tc.tile_pool(name="x", bufs=groups))
         junk_pool = ctx.enter_context(tc.tile_pool(name="junk", bufs=4))
         stat_pool = ctx.enter_context(tc.tile_pool(name="stat", bufs=6))
         y_pool = ctx.enter_context(tc.tile_pool(name="y", bufs=2 * GROUP))
@@ -52,7 +64,6 @@ def tile_transformerblocktpu_pa_t_kernel(
 
         x_tiles = {}
         rms_tiles = {}
-        rstd_tiles = {}
         y_tiles = {}
         yT_tiles = {}
         h_tiles = {}
@@ -62,8 +73,8 @@ def tile_transformerblocktpu_pa_t_kernel(
         stage_tiles = {}
 
         def load(g):
-            x_g = x_pool.tile([P, GROUP, FEATURES], BF16)
-            nc.sync.dma_start(out=x_g[:], in_=x_rows[:, g * GROUP : (g + 1) * GROUP, :])
+            x_g = x_pool.tile([P, sizes[g], FEATURES], BF16)
+            nc.sync.dma_start(out=x_g[:], in_=x_rows[:, firsts[g] : firsts[g] + sizes[g], :])
             x_tiles[g] = x_g
 
         load(0)
@@ -81,7 +92,7 @@ def tile_transformerblocktpu_pa_t_kernel(
                 out=w_plane[32 * quadrant : 32 * quadrant + 4, :].bitcast(I32),
                 in_=w_qkv_scales[0, 4 * quadrant : 4 * quadrant + 4, :].bitcast(I32),
             )
-        for g in range(1, GROUPS):
+        for g in range(1, groups):
             load(g)
         eps = const.tile([P, 1], F32)
         nc.vector.memset(eps[:], EPS)
@@ -91,8 +102,8 @@ def tile_transformerblocktpu_pa_t_kernel(
         make_identity(nc, ident[:])
 
         def statistics(g):
-            sumsq = stat_pool.tile([P, GROUP], F32)
-            for j in range(GROUP):
+            sumsq = stat_pool.tile([P, sizes[g]], F32)
+            for j in range(sizes[g]):
                 junk = junk_pool.tile([P, FEATURES], BF16)
                 nc.scalar.activation(
                     out=junk[:],
@@ -100,20 +111,19 @@ def tile_transformerblocktpu_pa_t_kernel(
                     func=ACT.Square,
                     accum_out=sumsq[:, j : j + 1],
                 )
-            rms = stat_pool.tile([P, GROUP], F32)
+            rms = stat_pool.tile([P, sizes[g]], F32)
             nc.scalar.activation(
                 out=rms[:], in_=sumsq[:], func=ACT.Sqrt, scale=1.0 / FEATURES, bias=eps[:]
             )
             rms_tiles[g] = rms
 
         def scale_rows(g):
-            rstd = stat_pool.tile([P, GROUP], F32)
+            rstd = stat_pool.tile([P, sizes[g]], F32)
             nc.vector.reciprocal(out=rstd[:], in_=rms_tiles[g][:])
-            rstd_tiles[g] = rstd
-            for j in range(GROUP):
+            for j in range(sizes[g]):
                 y = y_pool.tile([P, PACK, P], F32)
                 sorted_x = x_tiles[g][:, j, :].rearrange("r (c t) -> r t c", t=PACK)
-                if j == VECTOR_TILE:
+                if j == sizes[g] - 1:
                     nc.vector.tensor_scalar(
                         out=y[:], in0=sorted_x, scalar1=rstd[:, j : j + 1], scalar2=None, op0=ALU.mult
                     )
@@ -129,15 +139,15 @@ def tile_transformerblocktpu_pa_t_kernel(
                 y_tiles[(g, j)] = y
 
         def transpose(g):
-            for j in range(GROUP):
+            for j in range(sizes[g]):
                 yT = psum_t.tile([P, PACK, P], F32)
                 for t in range(PACK):
                     nc.tensor.transpose(yT[:, t, :], y_tiles[(g, j)][:, t, :], ident[:])
                 yT_tiles[(g, j)] = yT
 
         def apply_gain(g):
-            h = h_pool.tile([P, GROUP, P, PACK], BF16, align_bytes=64)
-            for j in range(GROUP):
+            h = h_pool.tile([P, sizes[g], P, PACK], BF16, align_bytes=64)
+            for j in range(sizes[g]):
                 nc.vector.tensor_tensor(
                     out=h[:, j, :, :],
                     in0=yT_tiles[(g, j)][:].rearrange("c t r -> c r t"),
@@ -147,8 +157,8 @@ def tile_transformerblocktpu_pa_t_kernel(
             h_tiles[g] = h
 
         def quantise(g):
-            codes = q_pool.tile([P, GROUP * P], U32, align_bytes=64)
-            plane = q_pool.tile([P, GROUP * P], U8, align_bytes=64)
+            codes = q_pool.tile([P, sizes[g] * P], U32, align_bytes=64)
+            plane = q_pool.tile([P, sizes[g] * P], U8, align_bytes=64)
             nc.vector.quantize_mx(
                 out=codes[:].bitcast(FP8X4),
                 scales=plane[:],
@@ -158,7 +168,7 @@ def tile_transformerblocktpu_pa_t_kernel(
             plane_tiles[g] = plane
 
         def project(g):
-            for j in range(GROUP):
+            for j in range(sizes[g]):
                 acc = psum_o.tile([P, N_OUT], F32)
                 rows = slice(j * P, (j + 1) * P)
                 for lo, hi in ((0, 256), (256, N_OUT)):
@@ -173,11 +183,12 @@ def tile_transformerblocktpu_pa_t_kernel(
                     )
                 acc_tiles[(g, j)] = acc
 
-        def evacuate(g):
-            stage = o_pool.tile([P, PROJECTIONS, GROUP, HEAD], F32)
-            for j in range(GROUP):
-                copy = nc.vector.tensor_copy if j == VECTOR_TILE else nc.scalar.copy
-                copy(
+        def evacuate(g, vector_helps):
+            stage = o_pool.tile([P, PROJECTIONS, sizes[g], HEAD], F32)
+            for j in range(sizes[g]):
+                by_vector = vector_helps and j == sizes[g] - 1
+                copy_out = nc.vector.tensor_copy if by_vector else nc.scalar.copy
+                copy_out(
                     out=stage[:, :, j, :],
                     in_=acc_tiles[(g, j)][:].rearrange("r (i d) -> r i d", i=PROJECTIONS),
                 )
@@ -186,22 +197,22 @@ def tile_transformerblocktpu_pa_t_kernel(
         def store(g):
             for i in range(PROJECTIONS):
                 nc.sync.dma_start(
-                    out=out_rows[i][:, g * GROUP : (g + 1) * GROUP, :],
+                    out=out_rows[i][:, firsts[g] : firsts[g] + sizes[g], :],
                     in_=stage_tiles[g][:, i, :, :],
                 )
 
-        for step in range(-3, GROUPS + 1):
-            if 0 <= step < GROUPS:
+        for step in range(-STATS_LEAD, groups + 1):
+            if 0 <= step < groups:
                 apply_gain(step)
-            if 0 <= step + 1 < GROUPS:
+            if 0 <= step + 1 < groups:
                 transpose(step + 1)
             if step >= 1:
-                evacuate(step - 1)
+                evacuate(step - 1, vector_helps=step + STATS_LEAD < groups)
                 store(step - 1)
-            if 0 <= step < GROUPS:
+            if 0 <= step < groups:
                 quantise(step)
                 project(step)
-            if 0 <= step + 2 < GROUPS:
-                scale_rows(step + 2)
-            if step + 3 < GROUPS:
-                statistics(step + 3)
+            if 0 <= step + SCALE_LEAD < groups:
+                scale_rows(step + SCALE_LEAD)
+            if step + STATS_LEAD < groups:
+                statistics(step + STATS_LEAD)

@@ -21,6 +21,9 @@ N_OUT = PROJECTIONS * HEAD
 TOKENS = 4 * 2048
 TILES = TOKENS // P
 GROUP = 4
+GROUPS = TILES // GROUP
+VECTOR_SCALES = 0
+VECTOR_EVACUATES = GROUP - 1
 EPS = 1e-6
 SCALE_LEAD = 2
 STATS_LEAD = 3
@@ -28,21 +31,10 @@ STATS_LEAD = 3
 FLOPS = 2 * TOKENS * FEATURES * N_OUT
 
 
-def group_sizes():
-    ramp = [1]
-    while sum(ramp) < GROUP:
-        ramp.append(sum(ramp))
-    full = [GROUP] * ((TILES - 2 * sum(ramp)) // GROUP)
-    return ramp + full + list(reversed(ramp))
-
-
 def tile_transformerblocktpu_pa_t_kernel(
     tc, x, rms1_scale, w_qkv_words, w_qkv_scales, out_0, out_1, out_2
 ):
     nc = tc.nc
-    sizes = group_sizes()
-    groups = len(sizes)
-    firsts = [sum(sizes[:g]) for g in range(groups)]
 
     x_rows = x.rearrange("b (q j) k -> (b q) j k", j=TILES)
     out_rows = [
@@ -52,7 +44,7 @@ def tile_transformerblocktpu_pa_t_kernel(
     with ExitStack() as ctx:
         ctx.enter_context(tc.manual_schedule())
         const = ctx.enter_context(tc.tile_pool(name="const", bufs=1))
-        x_pool = ctx.enter_context(tc.tile_pool(name="x", bufs=groups))
+        x_pool = ctx.enter_context(tc.tile_pool(name="x", bufs=GROUPS))
         junk_pool = ctx.enter_context(tc.tile_pool(name="junk", bufs=4))
         stat_pool = ctx.enter_context(tc.tile_pool(name="stat", bufs=6))
         y_pool = ctx.enter_context(tc.tile_pool(name="y", bufs=2 * GROUP))
@@ -63,7 +55,9 @@ def tile_transformerblocktpu_pa_t_kernel(
         psum_o = ctx.enter_context(tc.psum_pool(name="psum_o", bufs=GROUP))
 
         x_tiles = {}
+        sumsq_tiles = {}
         rms_tiles = {}
+        rstd_tiles = {}
         y_tiles = {}
         yT_tiles = {}
         h_tiles = {}
@@ -72,12 +66,18 @@ def tile_transformerblocktpu_pa_t_kernel(
         acc_tiles = {}
         stage_tiles = {}
 
-        def load(g):
-            x_g = x_pool.tile([P, sizes[g], FEATURES], BF16)
-            nc.sync.dma_start(out=x_g[:], in_=x_rows[:, firsts[g] : firsts[g] + sizes[g], :])
+        def load(g, pieces):
+            x_g = x_pool.tile([P, GROUP, FEATURES], BF16)
+            tiles = GROUP // pieces
+            for first in range(0, GROUP, tiles):
+                nc.sync.dma_start(
+                    out=x_g[:, first : first + tiles, :],
+                    in_=x_rows[:, g * GROUP + first : g * GROUP + first + tiles, :],
+                )
             x_tiles[g] = x_g
 
-        load(0)
+        load(0, pieces=GROUP)
+        load(1, pieces=1)
         gain = const.tile([P, PACK], BF16)
         nc.sync.dma_start(out=gain[:], in_=rms1_scale.rearrange("(c t) -> c t", t=PACK))
         w_codes = const.tile([P, PACK * N_OUT], U8, align_bytes=64)
@@ -92,8 +92,8 @@ def tile_transformerblocktpu_pa_t_kernel(
                 out=w_plane[32 * quadrant : 32 * quadrant + 4, :].bitcast(I32),
                 in_=w_qkv_scales[0, 4 * quadrant : 4 * quadrant + 4, :].bitcast(I32),
             )
-        for g in range(1, groups):
-            load(g)
+        for g in range(2, GROUPS):
+            load(g, pieces=1)
         eps = const.tile([P, 1], F32)
         nc.vector.memset(eps[:], EPS)
         warm = const.tile([P, 1], F32)
@@ -101,9 +101,9 @@ def tile_transformerblocktpu_pa_t_kernel(
         ident = const.tile([P, P], F32)
         make_identity(nc, ident[:])
 
-        def statistics(g):
-            sumsq = stat_pool.tile([P, sizes[g]], F32)
-            for j in range(sizes[g]):
+        def sum_squares(g):
+            sumsq = stat_pool.tile([P, GROUP], F32)
+            for j in range(GROUP):
                 junk = junk_pool.tile([P, FEATURES], BF16)
                 nc.scalar.activation(
                     out=junk[:],
@@ -111,19 +111,26 @@ def tile_transformerblocktpu_pa_t_kernel(
                     func=ACT.Square,
                     accum_out=sumsq[:, j : j + 1],
                 )
-            rms = stat_pool.tile([P, sizes[g]], F32)
+            sumsq_tiles[g] = sumsq
+
+        def root(g):
+            rms = stat_pool.tile([P, GROUP], F32)
             nc.scalar.activation(
-                out=rms[:], in_=sumsq[:], func=ACT.Sqrt, scale=1.0 / FEATURES, bias=eps[:]
+                out=rms[:], in_=sumsq_tiles[g][:], func=ACT.Sqrt, scale=1.0 / FEATURES, bias=eps[:]
             )
             rms_tiles[g] = rms
 
-        def scale_rows(g):
-            rstd = stat_pool.tile([P, sizes[g]], F32)
+        def invert(g):
+            rstd = stat_pool.tile([P, GROUP], F32)
             nc.vector.reciprocal(out=rstd[:], in_=rms_tiles[g][:])
-            for j in range(sizes[g]):
+            rstd_tiles[g] = rstd
+
+        def scale_rows(g):
+            rstd = rstd_tiles[g]
+            for j in range(GROUP):
                 y = y_pool.tile([P, PACK, P], F32)
                 sorted_x = x_tiles[g][:, j, :].rearrange("r (c t) -> r t c", t=PACK)
-                if j == sizes[g] - 1:
+                if j == VECTOR_SCALES:
                     nc.vector.tensor_scalar(
                         out=y[:], in0=sorted_x, scalar1=rstd[:, j : j + 1], scalar2=None, op0=ALU.mult
                     )
@@ -139,15 +146,15 @@ def tile_transformerblocktpu_pa_t_kernel(
                 y_tiles[(g, j)] = y
 
         def transpose(g):
-            for j in range(sizes[g]):
+            for j in range(GROUP):
                 yT = psum_t.tile([P, PACK, P], F32)
                 for t in range(PACK):
                     nc.tensor.transpose(yT[:, t, :], y_tiles[(g, j)][:, t, :], ident[:])
                 yT_tiles[(g, j)] = yT
 
         def apply_gain(g):
-            h = h_pool.tile([P, sizes[g], P, PACK], BF16, align_bytes=64)
-            for j in range(sizes[g]):
+            h = h_pool.tile([P, GROUP, P, PACK], BF16, align_bytes=64)
+            for j in range(GROUP):
                 nc.vector.tensor_tensor(
                     out=h[:, j, :, :],
                     in0=yT_tiles[(g, j)][:].rearrange("c t r -> c r t"),
@@ -157,8 +164,8 @@ def tile_transformerblocktpu_pa_t_kernel(
             h_tiles[g] = h
 
         def quantise(g):
-            codes = q_pool.tile([P, sizes[g] * P], U32, align_bytes=64)
-            plane = q_pool.tile([P, sizes[g] * P], U8, align_bytes=64)
+            codes = q_pool.tile([P, GROUP * P], U32, align_bytes=64)
+            plane = q_pool.tile([P, GROUP * P], U8, align_bytes=64)
             nc.vector.quantize_mx(
                 out=codes[:].bitcast(FP8X4),
                 scales=plane[:],
@@ -168,7 +175,7 @@ def tile_transformerblocktpu_pa_t_kernel(
             plane_tiles[g] = plane
 
         def project(g):
-            for j in range(sizes[g]):
+            for j in range(GROUP):
                 acc = psum_o.tile([P, N_OUT], F32)
                 rows = slice(j * P, (j + 1) * P)
                 for lo, hi in ((0, 256), (256, N_OUT)):
@@ -184,9 +191,9 @@ def tile_transformerblocktpu_pa_t_kernel(
                 acc_tiles[(g, j)] = acc
 
         def evacuate(g, vector_helps):
-            stage = o_pool.tile([P, PROJECTIONS, sizes[g], HEAD], F32)
-            for j in range(sizes[g]):
-                by_vector = vector_helps and j == sizes[g] - 1
+            stage = o_pool.tile([P, PROJECTIONS, GROUP, HEAD], F32)
+            for j in range(GROUP):
+                by_vector = vector_helps and j == VECTOR_EVACUATES
                 copy_out = nc.vector.tensor_copy if by_vector else nc.scalar.copy
                 copy_out(
                     out=stage[:, :, j, :],
@@ -197,22 +204,25 @@ def tile_transformerblocktpu_pa_t_kernel(
         def store(g):
             for i in range(PROJECTIONS):
                 nc.sync.dma_start(
-                    out=out_rows[i][:, firsts[g] : firsts[g] + sizes[g], :],
+                    out=out_rows[i][:, g * GROUP : (g + 1) * GROUP, :],
                     in_=stage_tiles[g][:, i, :, :],
                 )
 
-        for step in range(-STATS_LEAD, groups + 1):
-            if 0 <= step < groups:
+        for step in range(-STATS_LEAD, GROUPS + 1):
+            if 0 <= step < GROUPS:
                 apply_gain(step)
-            if 0 <= step + 1 < groups:
+            if 0 <= step + 1 < GROUPS:
                 transpose(step + 1)
             if step >= 1:
-                evacuate(step - 1, vector_helps=step + STATS_LEAD < groups)
+                evacuate(step - 1, vector_helps=step + STATS_LEAD < GROUPS)
                 store(step - 1)
-            if 0 <= step < groups:
+            if 0 <= step + SCALE_LEAD < GROUPS:
+                root(step + SCALE_LEAD)
+                invert(step + SCALE_LEAD)
+            if 0 <= step < GROUPS:
                 quantise(step)
                 project(step)
-            if 0 <= step + SCALE_LEAD < groups:
+            if 0 <= step + SCALE_LEAD < GROUPS:
                 scale_rows(step + SCALE_LEAD)
-            if step + STATS_LEAD < groups:
-                statistics(step + STATS_LEAD)
+            if step + STATS_LEAD < GROUPS:
+                sum_squares(step + STATS_LEAD)

@@ -101,17 +101,29 @@ def tile_transformerblocktpu_pa_t_kernel(
         ident = const.tile([P, P], F32)
         make_identity(nc, ident[:])
 
-        def sum_squares(g):
-            sumsq = stat_pool.tile([P, GROUP], F32)
-            for j in range(GROUP):
+        def sum_squares(g, j, by_vector=False):
+            if j == 0:
+                sumsq = stat_pool.tile([P, GROUP], F32)
+                sumsq_tiles[g] = sumsq
+            if by_vector:
+                junk_v = junk_pool.tile([P, FEATURES], BF16)
+                nc.vector.scalar_tensor_tensor(
+                    out=junk_v[:],
+                    in0=x_tiles[g][:, j, :],
+                    scalar=1.0,
+                    in1=x_tiles[g][:, j, :],
+                    op0=ALU.mult,
+                    op1=ALU.mult,
+                    accum_out=sumsq_tiles[g][:, j : j + 1],
+                )
+            else:
                 junk = junk_pool.tile([P, FEATURES], BF16)
                 nc.scalar.activation(
                     out=junk[:],
                     in_=x_tiles[g][:, j, :],
                     func=ACT.Square,
-                    accum_out=sumsq[:, j : j + 1],
+                    accum_out=sumsq_tiles[g][:, j : j + 1],
                 )
-            sumsq_tiles[g] = sumsq
 
         def root(g):
             rms = stat_pool.tile([P, GROUP], F32)
@@ -125,43 +137,43 @@ def tile_transformerblocktpu_pa_t_kernel(
             nc.vector.reciprocal(out=rstd[:], in_=rms_tiles[g][:])
             rstd_tiles[g] = rstd
 
-        def scale_rows(g):
+        def scale_rows(g, j, engine):
             rstd = rstd_tiles[g]
-            for j in range(GROUP):
-                y = y_pool.tile([P, PACK, P], F32)
-                sorted_x = x_tiles[g][:, j, :].rearrange("r (c t) -> r t c", t=PACK)
-                if j == VECTOR_SCALES:
-                    nc.vector.tensor_scalar(
-                        out=y[:], in0=sorted_x, scalar1=rstd[:, j : j + 1], scalar2=None, op0=ALU.mult
-                    )
-                else:
-                    nc.gpsimd.tensor_scalar(
-                        out=y[:],
-                        in0=sorted_x,
-                        scalar1=rstd[:, j : j + 1],
-                        scalar2=0.0,
-                        op0=ALU.mult,
-                        op1=ALU.add,
-                    )
-                y_tiles[(g, j)] = y
-
-        def transpose(g):
-            for j in range(GROUP):
-                yT = psum_t.tile([P, PACK, P], F32)
-                for t in range(PACK):
-                    nc.tensor.transpose(yT[:, t, :], y_tiles[(g, j)][:, t, :], ident[:])
-                yT_tiles[(g, j)] = yT
-
-        def apply_gain(g):
-            h = h_pool.tile([P, GROUP, P, PACK], BF16, align_bytes=64)
-            for j in range(GROUP):
-                nc.vector.tensor_tensor(
-                    out=h[:, j, :, :],
-                    in0=yT_tiles[(g, j)][:].rearrange("c t r -> c r t"),
-                    in1=gain[:].unsqueeze(1).to_broadcast([P, P, PACK]),
-                    op=ALU.mult,
+            y = y_pool.tile([P, PACK, P], F32)
+            sorted_x = x_tiles[g][:, j, :].rearrange("r (c t) -> r t c", t=PACK)
+            if engine == "vector":
+                nc.vector.tensor_scalar(
+                    out=y[:], in0=sorted_x, scalar1=rstd[:, j : j + 1], scalar2=None, op0=ALU.mult
                 )
-            h_tiles[g] = h
+            elif engine == "scalar":
+                nc.scalar.activation(out=y[:], in_=sorted_x, func=ACT.Copy, scale=rstd[:, j : j + 1])
+            else:
+                nc.gpsimd.tensor_scalar(
+                    out=y[:],
+                    in0=sorted_x,
+                    scalar1=rstd[:, j : j + 1],
+                    scalar2=0.0,
+                    op0=ALU.mult,
+                    op1=ALU.add,
+                )
+            y_tiles[(g, j)] = y
+
+        def transpose(g, j):
+            yT = psum_t.tile([P, PACK, P], F32)
+            for t in range(PACK):
+                nc.tensor.transpose(yT[:, t, :], y_tiles[(g, j)][:, t, :], ident[:])
+            yT_tiles[(g, j)] = yT
+
+        def apply_gain(g, j):
+            if j == 0:
+                h = h_pool.tile([P, GROUP, P, PACK], BF16, align_bytes=64)
+                h_tiles[g] = h
+            nc.vector.tensor_tensor(
+                out=h_tiles[g][:, j, :, :],
+                in0=yT_tiles[(g, j)][:].rearrange("c t r -> c r t"),
+                in1=gain[:].unsqueeze(1).to_broadcast([P, P, PACK]),
+                op=ALU.mult,
+            )
 
         def quantise(g):
             codes = q_pool.tile([P, GROUP * P], U32, align_bytes=64)
@@ -190,39 +202,87 @@ def tile_transformerblocktpu_pa_t_kernel(
                     )
                 acc_tiles[(g, j)] = acc
 
-        def evacuate(g, vector_helps):
-            stage = o_pool.tile([P, PROJECTIONS, GROUP, HEAD], F32)
-            for j in range(GROUP):
-                by_vector = vector_helps and j == VECTOR_EVACUATES
-                copy_out = nc.vector.tensor_copy if by_vector else nc.scalar.copy
-                copy_out(
-                    out=stage[:, :, j, :],
-                    in_=acc_tiles[(g, j)][:].rearrange("r (i d) -> r i d", i=PROJECTIONS),
-                )
-            stage_tiles[g] = stage
+        def evacuate(g, j, by_vector):
+            if j == 0:
+                stage = o_pool.tile([P, PROJECTIONS, GROUP, HEAD], F32)
+                stage_tiles[g] = stage
+            copy_out = nc.vector.tensor_copy if by_vector else nc.scalar.copy
+            copy_out(
+                out=stage_tiles[g][:, :, j, :],
+                in_=acc_tiles[(g, j)][:].rearrange("r (i d) -> r i d", i=PROJECTIONS),
+            )
 
-        def store(g):
+        def store(g, first, tiles):
             for i in range(PROJECTIONS):
                 nc.sync.dma_start(
-                    out=out_rows[i][:, g * GROUP : (g + 1) * GROUP, :],
-                    in_=stage_tiles[g][:, i, :, :],
+                    out=out_rows[i][:, g * GROUP + first : g * GROUP + first + tiles, :],
+                    in_=stage_tiles[g][:, i, first : first + tiles, :],
                 )
 
-        for step in range(-STATS_LEAD, GROUPS + 1):
-            if 0 <= step < GROUPS:
-                apply_gain(step)
-            if 0 <= step + 1 < GROUPS:
-                transpose(step + 1)
-            if step >= 1:
-                evacuate(step - 1, vector_helps=step + STATS_LEAD < GROUPS)
-                store(step - 1)
-            if 0 <= step + SCALE_LEAD < GROUPS:
+        LAST = GROUPS - 1
+
+        def scaler(g, j):
+            if g == LAST:
+                return "scalar" if j < 2 else "gpsimd"
+            return "vector" if j == VECTOR_SCALES else "gpsimd"
+
+        for j in range(GROUP):
+            sum_squares(0, j, by_vector=j % 2 == 1)
+        root(0)
+        invert(0)
+        for j in range(GROUP):
+            scale_rows(0, j, "vector")
+        for j in range(GROUP):
+            sum_squares(1, j)
+        for j in range(GROUP):
+            transpose(0, j)
+        root(1)
+        apply_gain(0, 0)
+        apply_gain(0, 1)
+        invert(1)
+        for j in range(GROUP):
+            scale_rows(1, j, "vector" if j < 2 else "gpsimd")
+        for j in range(GROUP):
+            sum_squares(2, j)
+        apply_gain(0, 2)
+        apply_gain(0, 3)
+        for j in range(GROUP):
+            transpose(1, j)
+        root(2)
+        invert(2)
+        quantise(0)
+        project(0)
+        for j in range(GROUP):
+            scale_rows(2, j, scaler(2, j))
+        for j in range(GROUP):
+            sum_squares(3, j)
+
+        for step in range(1, GROUPS + 1):
+            if step < GROUPS:
+                for j in range(GROUP):
+                    apply_gain(step, j)
+            if step + 1 < GROUPS:
+                for j in range(GROUP):
+                    transpose(step + 1, j)
+            if step - 1 < LAST:
+                vector_helps = step + STATS_LEAD < GROUPS
+                for j in range(GROUP):
+                    evacuate(step - 1, j, by_vector=vector_helps and j == VECTOR_EVACUATES)
+                store(step - 1, 0, GROUP)
+            else:
+                for first in range(0, GROUP, 2):
+                    evacuate(LAST, first, by_vector=False)
+                    evacuate(LAST, first + 1, by_vector=True)
+                    store(LAST, first, 2)
+            if step + SCALE_LEAD < GROUPS:
                 root(step + SCALE_LEAD)
                 invert(step + SCALE_LEAD)
-            if 0 <= step < GROUPS:
+            if step < GROUPS:
                 quantise(step)
                 project(step)
-            if 0 <= step + SCALE_LEAD < GROUPS:
-                scale_rows(step + SCALE_LEAD)
+            if step + SCALE_LEAD < GROUPS:
+                for j in range(GROUP):
+                    scale_rows(step + SCALE_LEAD, j, scaler(step + SCALE_LEAD, j))
             if step + STATS_LEAD < GROUPS:
-                sum_squares(step + STATS_LEAD)
+                for j in range(GROUP):
+                    sum_squares(step + STATS_LEAD, j)

@@ -26,7 +26,6 @@ VECTOR_SCALES = 0
 VECTOR_EVACUATES = GROUP - 1
 EPS = 1e-6
 SCALE_LEAD = 2
-STATS_LEAD = 3
 
 FLOPS = 2 * TOKENS * FEATURES * N_OUT
 
@@ -254,35 +253,35 @@ def tile_transformerblocktpu_pa_t_kernel(
         project(0)
         for j in range(GROUP):
             scale_rows(2, j, scaler(2, j))
-        for j in range(GROUP):
-            sum_squares(3, j)
 
         for step in range(1, GROUPS + 1):
+            ahead = step + SCALE_LEAD
             if step < GROUPS:
                 for j in range(GROUP):
                     apply_gain(step, j)
             if step + 1 < GROUPS:
                 for j in range(GROUP):
                     transpose(step + 1, j)
-            if step - 1 < LAST:
-                vector_helps = step + STATS_LEAD < GROUPS
+            if ahead < GROUPS:
                 for j in range(GROUP):
-                    evacuate(step - 1, j, by_vector=vector_helps and j == VECTOR_EVACUATES)
+                    sum_squares(ahead, j)
+            if step - 1 < LAST:
+                evacuate(step - 1, 0, by_vector=False)
+                if ahead < GROUPS:
+                    root(ahead)
+                for j in range(1, GROUP):
+                    evacuate(step - 1, j, by_vector=ahead < GROUPS and j == VECTOR_EVACUATES)
                 store(step - 1, 0, GROUP)
             else:
                 for first in range(0, GROUP, 2):
                     evacuate(LAST, first, by_vector=False)
                     evacuate(LAST, first + 1, by_vector=True)
                     store(LAST, first, 2)
-            if step + SCALE_LEAD < GROUPS:
-                root(step + SCALE_LEAD)
-                invert(step + SCALE_LEAD)
+            if ahead < GROUPS:
+                invert(ahead)
             if step < GROUPS:
                 quantise(step)
                 project(step)
-            if step + SCALE_LEAD < GROUPS:
+            if ahead < GROUPS:
                 for j in range(GROUP):
-                    scale_rows(step + SCALE_LEAD, j, scaler(step + SCALE_LEAD, j))
-            if step + STATS_LEAD < GROUPS:
-                for j in range(GROUP):
-                    sum_squares(step + STATS_LEAD, j)
+                    scale_rows(ahead, j, scaler(ahead, j))

@@ -174,19 +174,21 @@ def tile_transformerblocktpu_pa_t_kernel(
                 op=ALU.mult,
             )
 
-        def quantise(g):
-            codes = q_pool.tile([P, GROUP * P], U32, align_bytes=64)
-            plane = q_pool.tile([P, GROUP * P], U8, align_bytes=64)
+        def quantise(g, first=0, tiles=GROUP):
+            if first == 0:
+                codes = q_pool.tile([P, GROUP * P], U32, align_bytes=64)
+                plane = q_pool.tile([P, GROUP * P], U8, align_bytes=64)
+                code_tiles[g] = codes
+                plane_tiles[g] = plane
+            columns = slice(first * P, (first + tiles) * P)
             nc.vector.quantize_mx(
-                out=codes[:].bitcast(FP8X4),
-                scales=plane[:],
-                in_=h_tiles[g][:].rearrange("c j r t -> c (j r t)"),
+                out=code_tiles[g][:, columns].bitcast(FP8X4),
+                scales=plane_tiles[g][:, columns],
+                in_=h_tiles[g][:, first : first + tiles, :, :].rearrange("c j r t -> c (j r t)"),
             )
-            code_tiles[g] = codes
-            plane_tiles[g] = plane
 
-        def project(g):
-            for j in range(GROUP):
+        def project(g, first=0, tiles=GROUP):
+            for j in range(first, first + tiles):
                 acc = psum_o.tile([P, N_OUT], F32)
                 rows = slice(j * P, (j + 1) * P)
                 for lo, hi in ((0, 256), (256, N_OUT)):
@@ -254,7 +256,7 @@ def tile_transformerblocktpu_pa_t_kernel(
         for j in range(GROUP):
             scale_rows(2, j, scaler(2, j))
 
-        for step in range(1, GROUPS + 1):
+        for step in range(1, LAST):
             ahead = step + SCALE_LEAD
             if step < GROUPS:
                 for j in range(GROUP):
@@ -285,3 +287,20 @@ def tile_transformerblocktpu_pa_t_kernel(
             if ahead < GROUPS:
                 for j in range(GROUP):
                     scale_rows(ahead, j, scaler(ahead, j))
+
+        for j in range(GROUP - 1):
+            apply_gain(LAST, j)
+        for j in range(GROUP):
+            evacuate(LAST - 1, j, by_vector=False)
+        store(LAST - 1, 0, GROUP)
+        quantise(LAST, 0, 2)
+        project(LAST, 0, 2)
+        apply_gain(LAST, GROUP - 1)
+        quantise(LAST, 2, 2)
+        project(LAST, 2, 2)
+        evacuate(LAST, 0, by_vector=False)
+        evacuate(LAST, 1, by_vector=False)
+        store(LAST, 0, 2)
+        evacuate(LAST, 2, by_vector=False)
+        evacuate(LAST, 3, by_vector=True)
+        store(LAST, 2, 2)

@@ -256,7 +256,7 @@ def tile_transformerblocktpu_pa_t_kernel(
         for j in range(GROUP):
             scale_rows(2, j, scaler(2, j))
 
-        for step in range(1, LAST):
+        for step in range(1, LAST - 1):
             ahead = step + SCALE_LEAD
             if step < GROUPS:
                 for j in range(GROUP):
@@ -288,16 +288,24 @@ def tile_transformerblocktpu_pa_t_kernel(
                 for j in range(GROUP):
                     scale_rows(ahead, j, scaler(ahead, j))
 
-        for j in range(GROUP - 1):
-            apply_gain(LAST, j)
-        for j in range(GROUP):
-            evacuate(LAST - 1, j, by_vector=False)
-        store(LAST - 1, 0, GROUP)
-        quantise(LAST, 0, 2)
-        project(LAST, 0, 2)
-        apply_gain(LAST, GROUP - 1)
-        quantise(LAST, 2, 2)
-        project(LAST, 2, 2)
+        for g in (LAST - 1, LAST):
+            for j in range(GROUP - 1):
+                apply_gain(g, j)
+            if g < LAST:
+                for j in range(GROUP - 1):
+                    transpose(g + 1, j)
+            for j in range(GROUP):
+                evacuate(g - 1, j, by_vector=False)
+            store(g - 1, 0, GROUP)
+            quantise(g, 0, 2)
+            project(g, 0, 2)
+            apply_gain(g, GROUP - 1)
+            if g < LAST:
+                transpose(g + 1, GROUP - 1)
+            quantise(g, 2, 1)
+            project(g, 2, 1)
+            quantise(g, 3, 1)
+            project(g, 3, 1)
         evacuate(LAST, 0, by_vector=False)
         evacuate(LAST, 1, by_vector=False)
         store(LAST, 0, 2)

@@ -64,6 +64,7 @@ def tile_transformerblocktpu_pa_t_kernel(
         plane_tiles = {}
         acc_tiles = {}
         stage_tiles = {}
+        unsorted_tiles = set()
 
         def load(g, pieces):
             x_g = x_pool.tile([P, GROUP, FEATURES], BF16)
@@ -140,10 +141,19 @@ def tile_transformerblocktpu_pa_t_kernel(
             rstd = rstd_tiles[g]
             y = y_pool.tile([P, PACK, P], F32)
             sorted_x = x_tiles[g][:, j, :].rearrange("r (c t) -> r t c", t=PACK)
-            if engine == "vector":
+            if engine == "vector" and g < SCALE_LEAD:
                 nc.vector.tensor_scalar(
                     out=y[:], in0=sorted_x, scalar1=rstd[:, j : j + 1], scalar2=None, op0=ALU.mult
                 )
+            elif engine == "vector":
+                nc.vector.tensor_scalar(
+                    out=y[:].rearrange("r t c -> r (t c)"),
+                    in0=x_tiles[g][:, j, :],
+                    scalar1=rstd[:, j : j + 1],
+                    scalar2=None,
+                    op0=ALU.mult,
+                )
+                unsorted_tiles.add((g, j))
             elif engine == "scalar":
                 nc.scalar.activation(out=y[:], in_=sorted_x, func=ACT.Copy, scale=rstd[:, j : j + 1])
             else:
@@ -159,8 +169,13 @@ def tile_transformerblocktpu_pa_t_kernel(
 
         def transpose(g, j):
             yT = psum_t.tile([P, PACK, P], F32)
+            y = y_tiles[(g, j)]
+            if (g, j) in unsorted_tiles:
+                by_t = y[:].rearrange("r t c -> r (t c)").rearrange("r (c t) -> r t c", t=PACK)
+            else:
+                by_t = y[:]
             for t in range(PACK):
-                nc.tensor.transpose(yT[:, t, :], y_tiles[(g, j)][:, t, :], ident[:])
+                nc.tensor.transpose(yT[:, t, :], by_t[:, t, :], ident[:])
             yT_tiles[(g, j)] = yT
 
         def apply_gain(g, j):

from contextlib import ExitStack

import concourse.mybir as mybir
from concourse.masks import make_identity

F32 = mybir.dt.float32
BF16 = mybir.dt.bfloat16
I32 = mybir.dt.int32
U32 = mybir.dt.uint32
U8 = mybir.dt.uint8
FP8X4 = mybir.dt.float8_e4m3fn_x4
ALU = mybir.AluOpType
ACT = mybir.ActivationFunctionType

P = 128
PACK = 4
FEATURES = P * PACK
HEAD = 128
PROJECTIONS = 3
N_OUT = PROJECTIONS * HEAD
TOKENS = 4 * 2048
TILES = TOKENS // P
GROUP = 4
GROUPS = TILES // GROUP
VECTOR_SCALES = 0
VECTOR_EVACUATES = GROUP - 1
EPS = 1e-6
SCALE_LEAD = 2

FLOPS = 2 * TOKENS * FEATURES * N_OUT


def tile_transformerblocktpu_pa_t_kernel(
    tc, x, rms1_scale, w_qkv_words, w_qkv_scales, out_0, out_1, out_2
):
    nc = tc.nc

    x_rows = x.rearrange("b (q j) k -> (b q) j k", j=TILES)
    out_rows = [
        o.rearrange("b (q j) h d -> (b q) j (h d)", j=TILES) for o in (out_0, out_1, out_2)
    ]

    with ExitStack() as ctx:
        ctx.enter_context(tc.manual_schedule())
        const = ctx.enter_context(tc.tile_pool(name="const", bufs=1))
        x_pool = ctx.enter_context(tc.tile_pool(name="x", bufs=GROUPS))
        junk_pool = ctx.enter_context(tc.tile_pool(name="junk", bufs=4))
        stat_pool = ctx.enter_context(tc.tile_pool(name="stat", bufs=6))
        y_pool = ctx.enter_context(tc.tile_pool(name="y", bufs=2 * GROUP))
        h_pool = ctx.enter_context(tc.tile_pool(name="h", bufs=2))
        q_pool = ctx.enter_context(tc.tile_pool(name="q", bufs=3))
        o_pool = ctx.enter_context(tc.tile_pool(name="o", bufs=4))
        psum_t = ctx.enter_context(tc.psum_pool(name="psum_t", bufs=GROUP))
        psum_o = ctx.enter_context(tc.psum_pool(name="psum_o", bufs=GROUP))

        x_tiles = {}
        sumsq_tiles = {}
        rms_tiles = {}
        rstd_tiles = {}
        y_tiles = {}
        yT_tiles = {}
        h_tiles = {}
        code_tiles = {}
        plane_tiles = {}
        acc_tiles = {}
        stage_tiles = {}
        unsorted_tiles = set()

        def load(g, pieces):
            x_g = x_pool.tile([P, GROUP, FEATURES], BF16)
            tiles = GROUP // pieces
            for first in range(0, GROUP, tiles):
                nc.sync.dma_start(
                    out=x_g[:, first : first + tiles, :],
                    in_=x_rows[:, g * GROUP + first : g * GROUP + first + tiles, :],
                )
            x_tiles[g] = x_g

        load(0, pieces=GROUP)
        load(1, pieces=1)
        gain = const.tile([P, PACK], BF16)
        nc.sync.dma_start(out=gain[:], in_=rms1_scale.rearrange("(c t) -> c t", t=PACK))
        w_codes = const.tile([P, PACK * N_OUT], U8, align_bytes=64)
        nc.sync.dma_start(
            out=w_codes[:].bitcast(I32),
            in_=w_qkv_words[0].rearrange("p n t -> p (n t)").bitcast(I32),
        )
        w_plane = const.tile([P, N_OUT], U8, align_bytes=64)
        nc.vector.memset(w_plane[:].bitcast(I32), 0)
        for quadrant in range(4):
            nc.sync.dma_start(
                out=w_plane[32 * quadrant : 32 * quadrant + 4, :].bitcast(I32),
                in_=w_qkv_scales[0, 4 * quadrant : 4 * quadrant + 4, :].bitcast(I32),
            )
        for g in range(2, GROUPS):
            load(g, pieces=1)
        eps = const.tile([P, 1], F32)
        nc.vector.memset(eps[:], EPS)
        warm = const.tile([P, 1], F32)
        nc.scalar.activation(out=warm[:], in_=eps[:], func=ACT.Sqrt)
        ident = const.tile([P, P], F32)
        make_identity(nc, ident[:])

        def sum_squares(g, j, by_vector=False):
            if j == 0:
                sumsq = stat_pool.tile([P, GROUP], F32)
                sumsq_tiles[g] = sumsq
            if by_vector:
                junk_v = junk_pool.tile([P, FEATURES], BF16)
                nc.vector.scalar_tensor_tensor(
                    out=junk_v[:],
                    in0=x_tiles[g][:, j, :],
                    scalar=1.0,
                    in1=x_tiles[g][:, j, :],
                    op0=ALU.mult,
                    op1=ALU.mult,
                    accum_out=sumsq_tiles[g][:, j : j + 1],
                )
            else:
                junk = junk_pool.tile([P, FEATURES], BF16)
                nc.scalar.activation(
                    out=junk[:],
                    in_=x_tiles[g][:, j, :],
                    func=ACT.Square,
                    accum_out=sumsq_tiles[g][:, j : j + 1],
                )

        def root(g):
            rms = stat_pool.tile([P, GROUP], F32)
            nc.scalar.activation(
                out=rms[:], in_=sumsq_tiles[g][:], func=ACT.Sqrt, scale=1.0 / FEATURES, bias=eps[:]
            )
            rms_tiles[g] = rms

        def invert(g):
            rstd = stat_pool.tile([P, GROUP], F32)
            nc.vector.reciprocal(out=rstd[:], in_=rms_tiles[g][:])
            rstd_tiles[g] = rstd

        def scale_rows(g, j, engine):
            rstd = rstd_tiles[g]
            y = y_pool.tile([P, PACK, P], F32)
            sorted_x = x_tiles[g][:, j, :].rearrange("r (c t) -> r t c", t=PACK)
            if engine == "vector" and g < SCALE_LEAD:
                nc.vector.tensor_scalar(
                    out=y[:], in0=sorted_x, scalar1=rstd[:, j : j + 1], scalar2=None, op0=ALU.mult
                )
            elif engine == "vector":
                nc.vector.tensor_scalar(
                    out=y[:].rearrange("r t c -> r (t c)"),
                    in0=x_tiles[g][:, j, :],
                    scalar1=rstd[:, j : j + 1],
                    scalar2=None,
                    op0=ALU.mult,
                )
                unsorted_tiles.add((g, j))
            elif engine == "scalar":
                nc.scalar.activation(out=y[:], in_=sorted_x, func=ACT.Copy, scale=rstd[:, j : j + 1])
            else:
                nc.gpsimd.tensor_scalar(
                    out=y[:],
                    in0=sorted_x,
                    scalar1=rstd[:, j : j + 1],
                    scalar2=0.0,
                    op0=ALU.mult,
                    op1=ALU.add,
                )
            y_tiles[(g, j)] = y

        def transpose(g, j):
            yT = psum_t.tile([P, PACK, P], F32)
            y = y_tiles[(g, j)]
            if (g, j) in unsorted_tiles:
                by_t = y[:].rearrange("r t c -> r (t c)").rearrange("r (c t) -> r t c", t=PACK)
            else:
                by_t = y[:]
            for t in range(PACK):
                nc.tensor.transpose(yT[:, t, :], by_t[:, t, :], ident[:])
            yT_tiles[(g, j)] = yT

        def apply_gain(g, j):
            if j == 0:
                h = h_pool.tile([P, GROUP, P, PACK], BF16, align_bytes=64)
                h_tiles[g] = h
            nc.vector.tensor_tensor(
                out=h_tiles[g][:, j, :, :],
                in0=yT_tiles[(g, j)][:].rearrange("c t r -> c r t"),
                in1=gain[:].unsqueeze(1).to_broadcast([P, P, PACK]),
                op=ALU.mult,
            )

        def quantise(g, first=0, tiles=GROUP):
            if first == 0:
                codes = q_pool.tile([P, GROUP * P], U32, align_bytes=64)
                plane = q_pool.tile([P, GROUP * P], U8, align_bytes=64)
                code_tiles[g] = codes
                plane_tiles[g] = plane
            columns = slice(first * P, (first + tiles) * P)
            nc.vector.quantize_mx(
                out=code_tiles[g][:, columns].bitcast(FP8X4),
                scales=plane_tiles[g][:, columns],
                in_=h_tiles[g][:, first : first + tiles, :, :].rearrange("c j r t -> c (j r t)"),
            )

        def project(g, first=0, tiles=GROUP):
            for j in range(first, first + tiles):
                acc = psum_o.tile([P, N_OUT], F32)
                rows = slice(j * P, (j + 1) * P)
                for lo, hi in ((0, 256), (256, N_OUT)):
                    nc.tensor.matmul_mx(
                        out=acc[:, lo:hi],
                        lhsT=code_tiles[g][:, rows].bitcast(FP8X4),
                        lhsT_scale=plane_tiles[g][:, rows],
                        rhs=w_codes[:, PACK * lo : PACK * hi].bitcast(FP8X4),
                        rhs_scale=w_plane[:, lo:hi],
                        start=True,
                        stop=True,
                    )
                acc_tiles[(g, j)] = acc

        def evacuate(g, j, by_vector):
            if j == 0:
                stage = o_pool.tile([P, PROJECTIONS, GROUP, HEAD], F32)
                stage_tiles[g] = stage
            copy_out = nc.vector.tensor_copy if by_vector else nc.scalar.copy
            copy_out(
                out=stage_tiles[g][:, :, j, :],
                in_=acc_tiles[(g, j)][:].rearrange("r (i d) -> r i d", i=PROJECTIONS),
            )

        def store(g, first, tiles):
            for i in range(PROJECTIONS):
                nc.sync.dma_start(
                    out=out_rows[i][:, g * GROUP + first : g * GROUP + first + tiles, :],
                    in_=stage_tiles[g][:, i, first : first + tiles, :],
                )

        LAST = GROUPS - 1

        def scaler(g, j):
            if g == LAST:
                return "scalar" if j < 2 else "gpsimd"
            return "vector" if j == VECTOR_SCALES else "gpsimd"

        for j in range(GROUP):
            sum_squares(0, j, by_vector=j % 2 == 1)
        root(0)
        invert(0)
        for j in range(GROUP):
            scale_rows(0, j, "vector")
        for j in range(GROUP):
            sum_squares(1, j)
        for j in range(GROUP):
            transpose(0, j)
        root(1)
        apply_gain(0, 0)
        apply_gain(0, 1)
        invert(1)
        for j in range(GROUP):
            scale_rows(1, j, "vector" if j < 2 else "gpsimd")
        for j in range(GROUP):
            sum_squares(2, j)
        apply_gain(0, 2)
        apply_gain(0, 3)
        for j in range(GROUP):
            transpose(1, j)
        root(2)
        invert(2)
        quantise(0)
        project(0)
        for j in range(GROUP):
            scale_rows(2, j, scaler(2, j))

        for step in range(1, LAST - 1):
            ahead = step + SCALE_LEAD
            if step < GROUPS:
                for j in range(GROUP):
                    apply_gain(step, j)
            if step + 1 < GROUPS:
                for j in range(GROUP):
                    transpose(step + 1, j)
            if ahead < GROUPS:
                for j in range(GROUP):
                    sum_squares(ahead, j)
            if step - 1 < LAST:
                evacuate(step - 1, 0, by_vector=False)
                if ahead < GROUPS:
                    root(ahead)
                for j in range(1, GROUP):
                    evacuate(step - 1, j, by_vector=ahead < GROUPS and j == VECTOR_EVACUATES)
                store(step - 1, 0, GROUP)
            else:
                for first in range(0, GROUP, 2):
                    evacuate(LAST, first, by_vector=False)
                    evacuate(LAST, first + 1, by_vector=True)
                    store(LAST, first, 2)
            if ahead < GROUPS:
                invert(ahead)
            if step < GROUPS:
                quantise(step)
                project(step)
            if ahead < GROUPS:
                for j in range(GROUP):
                    scale_rows(ahead, j, scaler(ahead, j))

        for g in (LAST - 1, LAST):
            for j in range(GROUP - 1):
                apply_gain(g, j)
            if g < LAST:
                for j in range(GROUP - 1):
                    transpose(g + 1, j)
            for j in range(GROUP):
                evacuate(g - 1, j, by_vector=False)
            store(g - 1, 0, GROUP)
            quantise(g, 0, 2)
            project(g, 0, 2)
            apply_gain(g, GROUP - 1)
            if g < LAST:
                transpose(g + 1, GROUP - 1)
            quantise(g, 2, 1)
            project(g, 2, 1)
            quantise(g, 3, 1)
            project(g, 3, 1)
        evacuate(LAST, 0, by_vector=False)
        evacuate(LAST, 1, by_vector=False)
        store(LAST, 0, 2)
        evacuate(LAST, 2, by_vector=False)
        evacuate(LAST, 3, by_vector=True)
        store(LAST, 2, 2)
